import numpy as np
import ml_dtypes

BF16 = ml_dtypes.bfloat16


def bf(x):
    return np.asarray(x, np.float32).astype(BF16)


def f32(x):
    return np.asarray(x, np.float32)


def f64(x):
    return np.asarray(x).astype(np.float64)


def striped(idx):
    return np.tile(idx.reshape(-1, 16).T, (8, 1))


C, S, N = 1024, 512, 256
LOGIT_SCALE = 1.0 / 0.07


def setup_inputs():
    return {"x": f32(0.1 * np.random.standard_normal((C, S))), "own": f32(0.1 * np.random.standard_normal((C, N))), "offs": striped(np.random.permutation(np.tile(np.arange(S), 2))[:N])}


def reference(x, own, offs):
    idx = offs[:16].T.reshape(-1)
    s = f64(x)[:, idx] + f64(own)
    norm = np.sqrt(np.sum(s * s, axis=0, keepdims=True))
    return LOGIT_SCALE * s / norm

@@ -1,0 +1,48 @@
+import concourse.mybir as mybir
+
+F32 = mybir.dt.float32
+U16 = mybir.dt.uint16
+ADD = mybir.AluOpType.add
+MULT = mybir.AluOpType.mult
+ACT = mybir.ActivationFunctionType
+
+P = 128
+C, S, N = 1024, 512, 256
+BLOCKS = C // P
+TEMPERATURE = 0.07
+
+
+def tile_cliptrainloss_kernel(tc, x, own, offs, out):
+    nc = tc.nc
+    x_blocks = x.rearrange("(p b) s -> p b s", b=BLOCKS)
+    own_blocks = own.rearrange("(p b) n -> p b n", b=BLOCKS)
+    out_blocks = out.rearrange("(p b) n -> p b n", b=BLOCKS)
+
+    with tc.tile_pool(name="held", bufs=1) as held, tc.psum_pool(name="psum", bufs=1) as psum:
+        offsets = held.tile([P, N // 16], U16, name="offsets")
+        nc.sync.dma_start(offsets[:], offs)
+
+        bank = [held.tile([P, S], F32, name=f"bank{b}") for b in range(BLOCKS)]
+        own_sb = held.tile([P, BLOCKS, N], F32, name="own_sb")
+        for b in range(BLOCKS):
+            nc.sync.dma_start(bank[b][:], x_blocks[:, b, :])
+            nc.scalar.dma_start(own_sb[:, b, :], own_blocks[:, b, :])
+
+        ones = held.tile([P, P], F32, name="ones")
+        nc.vector.memset(ones[:], 1.0)
+
+        pooled = held.tile([P, BLOCKS, N], F32, name="pooled")
+        squares = held.tile([P, BLOCKS, N], F32, name="squares")
+        sumsq = psum.tile([P, N], F32, name="sumsq")
+        for b in range(BLOCKS):
+            nc.vector.tensor_tensor(pooled[:, b, :], bank[b][:].indirect(offsets[:]), own_sb[:, b, :], ADD)
+            nc.scalar.activation(squares[:, b, :], pooled[:, b, :], ACT.Square)
+            nc.tensor.matmul(sumsq[:], ones[:], squares[:, b, :], start=(b == 0), stop=(b == BLOCKS - 1))
+
+        factor = held.tile([P, N], F32, name="factor")
+        nc.scalar.activation(factor[:], sumsq[:], ACT.Abs_reciprocal_sqrt, scale=TEMPERATURE * TEMPERATURE)
+
+        result = held.tile([P, BLOCKS, N], F32, name="result")
+        for b in range(BLOCKS):
+            nc.vector.tensor_tensor(result[:, b, :], pooled[:, b, :], factor[:], MULT)
+            nc.sync.dma_start(out_blocks[:, b, :], result[:, b, :])

@@ -26,10 +26,13 @@ def tile_cliptrainloss_kernel(tc, x, own, offs, out):
         own_sb = held.tile([P, BLOCKS, N], F32, name="own_sb")
         for b in range(BLOCKS):
             nc.sync.dma_start(bank[b][:], x_blocks[:, b, :])
-            nc.scalar.dma_start(own_sb[:, b, :], own_blocks[:, b, :])
+            nc.sync.dma_start(own_sb[:, b, :], own_blocks[:, b, :])
 
         ones = held.tile([P, P], F32, name="ones")
         nc.vector.memset(ones[:], 1.0)
+
+        warm = held.tile([P, 1], F32, name="warm")
+        nc.scalar.activation(warm[:], ones[:, 0:1], ACT.Abs_reciprocal_sqrt)
 
         pooled = held.tile([P, BLOCKS, N], F32, name="pooled")
         squares = held.tile([P, BLOCKS, N], F32, name="squares")

@@ -26,7 +26,7 @@ def tile_cliptrainloss_kernel(tc, x, own, offs, out):
         own_sb = held.tile([P, BLOCKS, N], F32, name="own_sb")
         for b in range(BLOCKS):
             nc.sync.dma_start(bank[b][:], x_blocks[:, b, :])
-            nc.sync.dma_start(own_sb[:, b, :], own_blocks[:, b, :])
+            nc.scalar.dma_start(own_sb[:, b, :], own_blocks[:, b, :])
 
         ones = held.tile([P, P], F32, name="ones")
         nc.vector.memset(ones[:], 1.0)

@@ -1,6 +1,7 @@
 import concourse.mybir as mybir
 
 F32 = mybir.dt.float32
+BF16 = mybir.dt.bfloat16
 U16 = mybir.dt.uint16
 ADD = mybir.AluOpType.add
 MULT = mybir.AluOpType.mult
@@ -26,16 +27,16 @@ def tile_cliptrainloss_kernel(tc, x, own, offs, out):
         own_sb = held.tile([P, BLOCKS, N], F32, name="own_sb")
         for b in range(BLOCKS):
             nc.sync.dma_start(bank[b][:], x_blocks[:, b, :])
-            nc.scalar.dma_start(own_sb[:, b, :], own_blocks[:, b, :])
+            nc.sync.dma_start(own_sb[:, b, :], own_blocks[:, b, :])
 
-        ones = held.tile([P, P], F32, name="ones")
+        ones = held.tile([P, P], BF16, name="ones")
         nc.vector.memset(ones[:], 1.0)
 
         warm = held.tile([P, 1], F32, name="warm")
         nc.scalar.activation(warm[:], ones[:, 0:1], ACT.Abs_reciprocal_sqrt)
 
         pooled = held.tile([P, BLOCKS, N], F32, name="pooled")
-        squares = held.tile([P, BLOCKS, N], F32, name="squares")
+        squares = held.tile([P, BLOCKS, N], BF16, name="squares")
         sumsq = psum.tile([P, N], F32, name="sumsq")
         for b in range(BLOCKS):
             nc.vector.tensor_tensor(pooled[:, b, :], bank[b][:].indirect(offsets[:]), own_sb[:, b, :], ADD)

@@ -1,7 +1,6 @@
 import concourse.mybir as mybir
 
 F32 = mybir.dt.float32
-BF16 = mybir.dt.bfloat16
 U16 = mybir.dt.uint16
 ADD = mybir.AluOpType.add
 MULT = mybir.AluOpType.mult
@@ -10,6 +9,7 @@ ACT = mybir.ActivationFunctionType
 P = 128
 C, S, N = 1024, 512, 256
 BLOCKS = C // P
+OWN_GROUP = 4
 TEMPERATURE = 0.07
 
 
@@ -26,17 +26,18 @@ def tile_cliptrainloss_kernel(tc, x, own, offs, out):
         bank = [held.tile([P, S], F32, name=f"bank{b}") for b in range(BLOCKS)]
         own_sb = held.tile([P, BLOCKS, N], F32, name="own_sb")
         for b in range(BLOCKS):
+            if b % OWN_GROUP == 0:
+                nc.sync.dma_start(own_sb[:, b : b + OWN_GROUP, :], own_blocks[:, b : b + OWN_GROUP, :])
             nc.sync.dma_start(bank[b][:], x_blocks[:, b, :])
-            nc.sync.dma_start(own_sb[:, b, :], own_blocks[:, b, :])
 
-        ones = held.tile([P, P], BF16, name="ones")
+        ones = held.tile([P, P], F32, name="ones")
         nc.vector.memset(ones[:], 1.0)
 
         warm = held.tile([P, 1], F32, name="warm")
         nc.scalar.activation(warm[:], ones[:, 0:1], ACT.Abs_reciprocal_sqrt)
 
         pooled = held.tile([P, BLOCKS, N], F32, name="pooled")
-        squares = held.tile([P, BLOCKS, N], BF16, name="squares")
+        squares = held.tile([P, BLOCKS, N], F32, name="squares")
         sumsq = psum.tile([P, N], F32, name="sumsq")
         for b in range(BLOCKS):
             nc.vector.tensor_tensor(pooled[:, b, :], bank[b][:].indirect(offsets[:]), own_sb[:, b, :], ADD)

@@ -1,6 +1,7 @@
 import concourse.mybir as mybir
 
 F32 = mybir.dt.float32
+BF16 = mybir.dt.bfloat16
 U16 = mybir.dt.uint16
 ADD = mybir.AluOpType.add
 MULT = mybir.AluOpType.mult
@@ -10,6 +11,8 @@ P = 128
 C, S, N = 1024, 512, 256
 BLOCKS = C // P
 OWN_GROUP = 4
+PIECES = 2
+WIDTH = N // PIECES
 TEMPERATURE = 0.07
 
 
@@ -30,24 +33,34 @@ def tile_cliptrainloss_kernel(tc, x, own, offs, out):
                 nc.sync.dma_start(own_sb[:, b : b + OWN_GROUP, :], own_blocks[:, b : b + OWN_GROUP, :])
             nc.sync.dma_start(bank[b][:], x_blocks[:, b, :])
 
-        ones = held.tile([P, P], F32, name="ones")
+        ones = held.tile([P, P], BF16, name="ones")
         nc.vector.memset(ones[:], 1.0)
 
         warm = held.tile([P, 1], F32, name="warm")
         nc.scalar.activation(warm[:], ones[:, 0:1], ACT.Abs_reciprocal_sqrt)
 
+        columns = [slice(k * WIDTH, (k + 1) * WIDTH) for k in range(PIECES)]
+        piece = [offsets[:, k * (WIDTH // 16) : (k + 1) * (WIDTH // 16)] for k in range(PIECES)]
+
         pooled = held.tile([P, BLOCKS, N], F32, name="pooled")
-        squares = held.tile([P, BLOCKS, N], F32, name="squares")
-        sumsq = psum.tile([P, N], F32, name="sumsq")
+        squares = held.tile([P, BLOCKS, N], BF16, name="squares")
+        sumsq = [psum.tile([P, WIDTH], F32, name=f"sumsq{k}") for k in range(PIECES)]
         for b in range(BLOCKS):
-            nc.vector.tensor_tensor(pooled[:, b, :], bank[b][:].indirect(offsets[:]), own_sb[:, b, :], ADD)
-            nc.scalar.activation(squares[:, b, :], pooled[:, b, :], ACT.Square)
-            nc.tensor.matmul(sumsq[:], ones[:], squares[:, b, :], start=(b == 0), stop=(b == BLOCKS - 1))
+            for k in range(PIECES):
+                cols = columns[k]
+                nc.vector.tensor_tensor(pooled[:, b, cols], bank[b][:].indirect(piece[k]), own_sb[:, b, cols], ADD)
+                nc.scalar.activation(squares[:, b, cols], pooled[:, b, cols], ACT.Square)
+                nc.tensor.matmul(sumsq[k][:], ones[:], squares[:, b, cols], start=(b == 0), stop=(b == BLOCKS - 1))
 
         factor = held.tile([P, N], F32, name="factor")
-        nc.scalar.activation(factor[:], sumsq[:], ACT.Abs_reciprocal_sqrt, scale=TEMPERATURE * TEMPERATURE)
+        for k in range(PIECES):
+            nc.scalar.activation(
+                factor[:, columns[k]], sumsq[k][:], ACT.Abs_reciprocal_sqrt, scale=TEMPERATURE * TEMPERATURE
+            )
 
         result = held.tile([P, BLOCKS, N], F32, name="result")
         for b in range(BLOCKS):
-            nc.vector.tensor_tensor(result[:, b, :], pooled[:, b, :], factor[:], MULT)
+            for k in range(PIECES):
+                cols = columns[k]
+                nc.vector.tensor_tensor(result[:, b, cols], pooled[:, b, cols], factor[:, cols], MULT)
             nc.sync.dma_start(out_blocks[:, b, :], result[:, b, :])

@@ -13,6 +13,7 @@ BLOCKS = C // P
 OWN_GROUP = 4
 PIECES = 2
 WIDTH = N // PIECES
+OUT_GROUP = 2
 TEMPERATURE = 0.07
 
 
@@ -59,8 +60,14 @@ def tile_cliptrainloss_kernel(tc, x, own, offs, out):
             )
 
         result = held.tile([P, BLOCKS, N], F32, name="result")
-        for b in range(BLOCKS):
+        for b in range(0, BLOCKS, OUT_GROUP):
+            group = slice(b, b + OUT_GROUP)
             for k in range(PIECES):
                 cols = columns[k]
-                nc.vector.tensor_tensor(result[:, b, cols], pooled[:, b, cols], factor[:, cols], MULT)
-            nc.sync.dma_start(out_blocks[:, b, :], result[:, b, :])
+                nc.vector.tensor_tensor(
+                    result[:, group, cols],
+                    pooled[:, group, cols],
+                    factor[:, cols].unsqueeze(1).to_broadcast([P, OUT_GROUP, WIDTH]),
+                    MULT,
+                )
+            nc.sync.dma_start(out_blocks[:, group, :], result[:, group, :])

@@ -41,17 +41,26 @@ def tile_cliptrainloss_kernel(tc, x, own, offs, out):
         nc.scalar.activation(warm[:], ones[:, 0:1], ACT.Abs_reciprocal_sqrt)
 
         columns = [slice(k * WIDTH, (k + 1) * WIDTH) for k in range(PIECES)]
-        piece = [offsets[:, k * (WIDTH // 16) : (k + 1) * (WIDTH // 16)] for k in range(PIECES)]
 
         pooled = held.tile([P, BLOCKS, N], F32, name="pooled")
         squares = held.tile([P, BLOCKS, N], BF16, name="squares")
         sumsq = [psum.tile([P, WIDTH], F32, name=f"sumsq{k}") for k in range(PIECES)]
-        for b in range(BLOCKS):
+
+        def look_up(b, cols):
+            entries = offsets[:, cols.start // 16 : cols.stop // 16]
+            nc.vector.tensor_tensor(pooled[:, b, cols], bank[b][:].indirect(entries), own_sb[:, b, cols], ADD)
+            nc.scalar.activation(squares[:, b, cols], pooled[:, b, cols], ACT.Square)
+
+        def add_up(b, k):
+            nc.tensor.matmul(sumsq[k][:], ones[:], squares[:, b, columns[k]], start=(b == 0), stop=(b == BLOCKS - 1))
+
+        for b in range(BLOCKS - 1):
+            look_up(b, slice(0, N))
             for k in range(PIECES):
-                cols = columns[k]
-                nc.vector.tensor_tensor(pooled[:, b, cols], bank[b][:].indirect(piece[k]), own_sb[:, b, cols], ADD)
-                nc.scalar.activation(squares[:, b, cols], pooled[:, b, cols], ACT.Square)
-                nc.tensor.matmul(sumsq[k][:], ones[:], squares[:, b, cols], start=(b == 0), stop=(b == BLOCKS - 1))
+                add_up(b, k)
+        for k in range(PIECES):
+            look_up(BLOCKS - 1, columns[k])
+            add_up(BLOCKS - 1, k)
 
         factor = held.tile([P, N], F32, name="factor")
         for k in range(PIECES):

@@ -11,7 +11,7 @@ P = 128
 C, S, N = 1024, 512, 256
 BLOCKS = C // P
 OWN_GROUP = 4
-PIECES = 2
+PIECES = 4
 WIDTH = N // PIECES
 OUT_GROUP = 2
 TEMPERATURE = 0.07
@@ -54,29 +54,31 @@ def tile_cliptrainloss_kernel(tc, x, own, offs, out):
         def add_up(b, k):
             nc.tensor.matmul(sumsq[k][:], ones[:], squares[:, b, columns[k]], start=(b == 0), stop=(b == BLOCKS - 1))
 
-        for b in range(BLOCKS - 1):
-            look_up(b, slice(0, N))
-            for k in range(PIECES):
-                add_up(b, k)
-        for k in range(PIECES):
-            look_up(BLOCKS - 1, columns[k])
-            add_up(BLOCKS - 1, k)
-
-        factor = held.tile([P, N], F32, name="factor")
-        for k in range(PIECES):
+        def norm_factor(k):
             nc.scalar.activation(
                 factor[:, columns[k]], sumsq[k][:], ACT.Abs_reciprocal_sqrt, scale=TEMPERATURE * TEMPERATURE
             )
 
+        for b in range(BLOCKS - 1):
+            look_up(b, slice(0, N))
+            for k in range(PIECES):
+                add_up(b, k)
+        factor = held.tile([P, N], F32, name="factor")
+        for k in range(PIECES):
+            look_up(BLOCKS - 1, columns[k])
+            add_up(BLOCKS - 1, k)
+            if k > 0:
+                norm_factor(k - 1)
+        norm_factor(PIECES - 1)
+
         result = held.tile([P, BLOCKS, N], F32, name="result")
         for b in range(0, BLOCKS, OUT_GROUP):
             group = slice(b, b + OUT_GROUP)
-            for k in range(PIECES):
-                cols = columns[k]
+            for cols in columns if b == 0 else [slice(0, N)]:
                 nc.vector.tensor_tensor(
                     result[:, group, cols],
                     pooled[:, group, cols],
-                    factor[:, cols].unsqueeze(1).to_broadcast([P, OUT_GROUP, WIDTH]),
+                    factor[:, cols].unsqueeze(1).to_broadcast([P, OUT_GROUP, cols.stop - cols.start]),
                     MULT,
                 )
             nc.sync.dma_start(out_blocks[:, group, :], result[:, group, :])

@@ -49,6 +49,8 @@ def tile_cliptrainloss_kernel(tc, x, own, offs, out):
         def look_up(b, cols):
             entries = offsets[:, cols.start // 16 : cols.stop // 16]
             nc.vector.tensor_tensor(pooled[:, b, cols], bank[b][:].indirect(entries), own_sb[:, b, cols], ADD)
+
+        def square(b, cols):
             nc.scalar.activation(squares[:, b, cols], pooled[:, b, cols], ACT.Square)
 
         def add_up(b, k):
@@ -59,13 +61,19 @@ def tile_cliptrainloss_kernel(tc, x, own, offs, out):
                 factor[:, columns[k]], sumsq[k][:], ACT.Abs_reciprocal_sqrt, scale=TEMPERATURE * TEMPERATURE
             )
 
-        for b in range(BLOCKS - 1):
+        for b in range(BLOCKS - 2):
             look_up(b, slice(0, N))
+            square(b, slice(0, N))
             for k in range(PIECES):
                 add_up(b, k)
+        look_up(BLOCKS - 2, slice(0, N))
+        for k in range(PIECES):
+            square(BLOCKS - 2, columns[k])
+            add_up(BLOCKS - 2, k)
         factor = held.tile([P, N], F32, name="factor")
         for k in range(PIECES):
             look_up(BLOCKS - 1, columns[k])
+            square(BLOCKS - 1, columns[k])
             add_up(BLOCKS - 1, k)
             if k > 0:
                 norm_factor(k - 1)

@@ -25,7 +25,6 @@ def tile_cliptrainloss_kernel(tc, x, own, offs, out):
 
     with tc.tile_pool(name="held", bufs=1) as held, tc.psum_pool(name="psum", bufs=1) as psum:
         offsets = held.tile([P, N // 16], U16, name="offsets")
-        nc.sync.dma_start(offsets[:], offs)
 
         bank = [held.tile([P, S], F32, name=f"bank{b}") for b in range(BLOCKS)]
         own_sb = held.tile([P, BLOCKS, N], F32, name="own_sb")
@@ -33,6 +32,8 @@ def tile_cliptrainloss_kernel(tc, x, own, offs, out):
             if b % OWN_GROUP == 0:
                 nc.sync.dma_start(own_sb[:, b : b + OWN_GROUP, :], own_blocks[:, b : b + OWN_GROUP, :])
             nc.sync.dma_start(bank[b][:], x_blocks[:, b, :])
+            if b == 0:
+                nc.sync.dma_start(offsets[:], offs)
 
         ones = held.tile([P, P], BF16, name="ones")
         nc.vector.memset(ones[:], 1.0)

@@ -10,7 +10,7 @@ ACT = mybir.ActivationFunctionType
 P = 128
 C, S, N = 1024, 512, 256
 BLOCKS = C // P
-OWN_GROUP = 4
+OWN_FIRST = 6
 PIECES = 4
 WIDTH = N // PIECES
 OUT_GROUP = 2
@@ -29,8 +29,10 @@ def tile_cliptrainloss_kernel(tc, x, own, offs, out):
         bank = [held.tile([P, S], F32, name=f"bank{b}") for b in range(BLOCKS)]
         own_sb = held.tile([P, BLOCKS, N], F32, name="own_sb")
         for b in range(BLOCKS):
-            if b % OWN_GROUP == 0:
-                nc.sync.dma_start(own_sb[:, b : b + OWN_GROUP, :], own_blocks[:, b : b + OWN_GROUP, :])
+            if b == 0:
+                nc.sync.dma_start(own_sb[:, :OWN_FIRST, :], own_blocks[:, :OWN_FIRST, :])
+            if b == OWN_FIRST:
+                nc.sync.dma_start(own_sb[:, OWN_FIRST:, :], own_blocks[:, OWN_FIRST:, :])
             nc.sync.dma_start(bank[b][:], x_blocks[:, b, :])
             if b == 0:
                 nc.sync.dma_start(offsets[:], offs)
@@ -51,8 +53,11 @@ def tile_cliptrainloss_kernel(tc, x, own, offs, out):
             entries = offsets[:, cols.start // 16 : cols.stop // 16]
             nc.vector.tensor_tensor(pooled[:, b, cols], bank[b][:].indirect(entries), own_sb[:, b, cols], ADD)
 
-        def square(b, cols):
+        def square_on_scalar(b, cols):
             nc.scalar.activation(squares[:, b, cols], pooled[:, b, cols], ACT.Square)
+
+        def square_on_vector(b, cols):
+            nc.vector.tensor_tensor(squares[:, b, cols], pooled[:, b, cols], pooled[:, b, cols], MULT)
 
         def add_up(b, k):
             nc.tensor.matmul(sumsq[k][:], ones[:], squares[:, b, columns[k]], start=(b == 0), stop=(b == BLOCKS - 1))
@@ -64,17 +69,20 @@ def tile_cliptrainloss_kernel(tc, x, own, offs, out):
 
         for b in range(BLOCKS - 2):
             look_up(b, slice(0, N))
-            square(b, slice(0, N))
+            square_on_scalar(b, slice(0, N))
             for k in range(PIECES):
                 add_up(b, k)
         look_up(BLOCKS - 2, slice(0, N))
         for k in range(PIECES):
-            square(BLOCKS - 2, columns[k])
+            square_on_scalar(BLOCKS - 2, columns[k])
             add_up(BLOCKS - 2, k)
         factor = held.tile([P, N], F32, name="factor")
         for k in range(PIECES):
             look_up(BLOCKS - 1, columns[k])
-            square(BLOCKS - 1, columns[k])
+            if k < PIECES - 1:
+                square_on_scalar(BLOCKS - 1, columns[k])
+            else:
+                square_on_vector(BLOCKS - 1, columns[k])
             add_up(BLOCKS - 1, k)
             if k > 0:
                 norm_factor(k - 1)

import concourse.mybir as mybir

F32 = mybir.dt.float32
BF16 = mybir.dt.bfloat16
U16 = mybir.dt.uint16
ADD = mybir.AluOpType.add
MULT = mybir.AluOpType.mult
ACT = mybir.ActivationFunctionType

P = 128
C, S, N = 1024, 512, 256
BLOCKS = C // P
OWN_FIRST = 6
PIECES = 4
WIDTH = N // PIECES
OUT_GROUP = 2
TEMPERATURE = 0.07


def tile_cliptrainloss_kernel(tc, x, own, offs, out):
    nc = tc.nc
    x_blocks = x.rearrange("(p b) s -> p b s", b=BLOCKS)
    own_blocks = own.rearrange("(p b) n -> p b n", b=BLOCKS)
    out_blocks = out.rearrange("(p b) n -> p b n", b=BLOCKS)

    with tc.tile_pool(name="held", bufs=1) as held, tc.psum_pool(name="psum", bufs=1) as psum:
        offsets = held.tile([P, N // 16], U16, name="offsets")

        bank = [held.tile([P, S], F32, name=f"bank{b}") for b in range(BLOCKS)]
        own_sb = held.tile([P, BLOCKS, N], F32, name="own_sb")
        for b in range(BLOCKS):
            if b == 0:
                nc.sync.dma_start(own_sb[:, :OWN_FIRST, :], own_blocks[:, :OWN_FIRST, :])
            if b == OWN_FIRST:
                nc.sync.dma_start(own_sb[:, OWN_FIRST:, :], own_blocks[:, OWN_FIRST:, :])
            nc.sync.dma_start(bank[b][:], x_blocks[:, b, :])
            if b == 0:
                nc.sync.dma_start(offsets[:], offs)

        ones = held.tile([P, P], BF16, name="ones")
        nc.vector.memset(ones[:], 1.0)

        warm = held.tile([P, 1], F32, name="warm")
        nc.scalar.activation(warm[:], ones[:, 0:1], ACT.Abs_reciprocal_sqrt)

        columns = [slice(k * WIDTH, (k + 1) * WIDTH) for k in range(PIECES)]

        pooled = held.tile([P, BLOCKS, N], F32, name="pooled")
        squares = held.tile([P, BLOCKS, N], BF16, name="squares")
        sumsq = [psum.tile([P, WIDTH], F32, name=f"sumsq{k}") for k in range(PIECES)]

        def look_up(b, cols):
            entries = offsets[:, cols.start // 16 : cols.stop // 16]
            nc.vector.tensor_tensor(pooled[:, b, cols], bank[b][:].indirect(entries), own_sb[:, b, cols], ADD)

        def square_on_scalar(b, cols):
            nc.scalar.activation(squares[:, b, cols], pooled[:, b, cols], ACT.Square)

        def square_on_vector(b, cols):
            nc.vector.tensor_tensor(squares[:, b, cols], pooled[:, b, cols], pooled[:, b, cols], MULT)

        def add_up(b, k):
            nc.tensor.matmul(sumsq[k][:], ones[:], squares[:, b, columns[k]], start=(b == 0), stop=(b == BLOCKS - 1))

        def norm_factor(k):
            nc.scalar.activation(
                factor[:, columns[k]], sumsq[k][:], ACT.Abs_reciprocal_sqrt, scale=TEMPERATURE * TEMPERATURE
            )

        for b in range(BLOCKS - 2):
            look_up(b, slice(0, N))
            square_on_scalar(b, slice(0, N))
            for k in range(PIECES):
                add_up(b, k)
        look_up(BLOCKS - 2, slice(0, N))
        for k in range(PIECES):
            square_on_scalar(BLOCKS - 2, columns[k])
            add_up(BLOCKS - 2, k)
        factor = held.tile([P, N], F32, name="factor")
        for k in range(PIECES):
            look_up(BLOCKS - 1, columns[k])
            if k < PIECES - 1:
                square_on_scalar(BLOCKS - 1, columns[k])
            else:
                square_on_vector(BLOCKS - 1, columns[k])
            add_up(BLOCKS - 1, k)
            if k > 0:
                norm_factor(k - 1)
        norm_factor(PIECES - 1)

        result = held.tile([P, BLOCKS, N], F32, name="result")
        for b in range(0, BLOCKS, OUT_GROUP):
            group = slice(b, b + OUT_GROUP)
            for cols in columns if b == 0 else [slice(0, N)]:
                nc.vector.tensor_tensor(
                    result[:, group, cols],
                    pooled[:, group, cols],
                    factor[:, cols].unsqueeze(1).to_broadcast([P, OUT_GROUP, cols.stop - cols.start]),
                    MULT,
                )
            nc.sync.dma_start(out_blocks[:, group, :], result[:, group, :])
